import numpy as np
import ml_dtypes

BF16 = ml_dtypes.bfloat16


def bf(x):
    return np.asarray(x, np.float32).astype(BF16)


def f32(x):
    return np.asarray(x, np.float32)


def f64(x):
    return np.asarray(x).astype(np.float64)


def striped(idx):
    return np.tile(idx.reshape(-1, 16).T, (8, 1))


C, S, N = 512, 1024, 128
BIT = 4
QMAX = float(2 ** (BIT - 1) - 1)
HALF_STEP = 0.5 / QMAX


def setup_inputs():
    return {"q_weight": f32(np.random.standard_normal((C, S))), "noise": f32(np.random.standard_normal((C, S))), "alpha": f32(np.random.uniform(0.5, 3.0, (C, 1))), "fp_weight": f32(np.random.standard_normal((C, N))), "offs": striped(np.random.permutation(S)[:N])}


def reference(q_weight, noise, alpha, fp_weight, offs):
    idx = offs[:16].T.reshape(-1)
    w = f64(q_weight)
    a = f64(alpha)
    wn = w + f64(noise) * a * HALF_STEP
    wn = np.where(w <= -a, -a, wn)
    wn = np.where(w >= a, a, wn)
    out = wn.copy()
    out[:, idx] = f64(fp_weight)
    return out

@@ -1,0 +1,58 @@
+import concourse.mybir as mybir
+
+F32 = mybir.dt.float32
+U16 = mybir.dt.uint16
+ALU = mybir.AluOpType
+ACT = mybir.ActivationFunctionType
+
+P = 128
+C, S, N = 512, 1024, 128
+BLOCKS = C // P
+HALF_STEP = 0.5 / 7.0
+
+
+def tile_linear_kernel(tc, q_weight, noise, alpha, fp_weight, offs, out):
+    nc = tc.nc
+
+    q_rows = q_weight.rearrange("(p n) s -> p n s", n=BLOCKS)
+    noise_rows = noise.rearrange("(p n) s -> p n s", n=BLOCKS)
+    out_rows = out.rearrange("(p n) s -> p n s", n=BLOCKS)
+
+    with (
+        tc.tile_pool(name="held", bufs=1) as held,
+        tc.tile_pool(name="blocks", bufs=BLOCKS) as blocks,
+    ):
+        offsets = held.tile([P, N // 16], U16, name="offsets")
+        nc.sync.dma_start(offsets[:], offs)
+        alpha_t = held.tile([P, BLOCKS], F32, name="alpha_t")
+        nc.sync.dma_start(alpha_t[:], alpha.rearrange("(p n) one -> p (n one)", n=BLOCKS))
+        outliers = held.tile([P, BLOCKS * N], F32, name="outliers")
+
+        neg_alpha = held.tile([P, BLOCKS], F32, name="neg_alpha")
+        nc.vector.tensor_scalar_mul(neg_alpha[:], alpha_t[:], -1.0)
+        half_step = held.tile([P, BLOCKS], F32, name="half_step")
+        nc.vector.tensor_scalar_mul(half_step[:], alpha_t[:], HALF_STEP)
+
+        for n in range(BLOCKS):
+            a = alpha_t[:, n : n + 1]
+
+            q = blocks.tile([P, S], F32, name="q")
+            nc.sync.dma_start(q[:], q_rows[:, n, :])
+            z = blocks.tile([P, S], F32, name="z")
+            nc.sync.dma_start(z[:], noise_rows[:, n, :])
+            if n == 0:
+                nc.sync.dma_start(outliers[:], fp_weight.rearrange("(p n) j -> p (n j)", n=BLOCKS))
+
+            q_abs = blocks.tile([P, S], F32, name="q_abs")
+            nc.scalar.activation(q_abs[:], q[:], ACT.Abs)
+            clipped = blocks.tile([P, S], F32, name="clipped")
+            nc.vector.tensor_scalar(clipped[:], q[:], a, neg_alpha[:, n : n + 1], ALU.min, ALU.max)
+            kept = blocks.tile([P, S], F32, name="kept")
+            nc.vector.scalar_tensor_tensor(kept[:], q_abs[:], a, z[:], ALU.is_lt, ALU.mult)
+            wn = blocks.tile([P, S], F32, name="wn")
+            nc.vector.scalar_tensor_tensor(
+                wn[:], kept[:], half_step[:, n : n + 1], clipped[:], ALU.mult, ALU.add
+            )
+
+            nc.scalar.activation(wn[:].indirect(offsets[:]), outliers[:, n * N : (n + 1) * N], ACT.Copy)
+            nc.sync.dma_start(out_rows[:, n, :], wn[:])

@@ -33,15 +33,22 @@ def tile_linear_kernel(tc, q_weight, noise, alpha, fp_weight, offs, out):
         half_step = held.tile([P, BLOCKS], F32, name="half_step")
         nc.vector.tensor_scalar_mul(half_step[:], alpha_t[:], HALF_STEP)
 
+        q_tiles = []
+        z_tiles = []
         for n in range(BLOCKS):
-            a = alpha_t[:, n : n + 1]
-
             q = blocks.tile([P, S], F32, name="q")
             nc.sync.dma_start(q[:], q_rows[:, n, :])
+            q_tiles.append(q)
             z = blocks.tile([P, S], F32, name="z")
             nc.sync.dma_start(z[:], noise_rows[:, n, :])
+            z_tiles.append(z)
             if n == 0:
                 nc.sync.dma_start(outliers[:], fp_weight.rearrange("(p n) j -> p (n j)", n=BLOCKS))
+
+        for n in range(BLOCKS):
+            a = alpha_t[:, n : n + 1]
+            q = q_tiles[n]
+            z = z_tiles[n]
 
             q_abs = blocks.tile([P, S], F32, name="q_abs")
             nc.scalar.activation(q_abs[:], q[:], ACT.Abs)

@@ -9,6 +9,13 @@ P = 128
 C, S, N = 512, 1024, 128
 BLOCKS = C // P
 HALF_STEP = 0.5 / 7.0
+FIRST_BLOCK_EDGES = (0, S // 4, S // 2, S)
+BLOCK_EDGES = (0, S)
+
+
+def column_pieces(n):
+    edges = FIRST_BLOCK_EDGES if n == 0 else BLOCK_EDGES
+    return [slice(lo, hi) for lo, hi in zip(edges[:-1], edges[1:])]
 
 
 def tile_linear_kernel(tc, q_weight, noise, alpha, fp_weight, offs, out):
@@ -22,44 +29,49 @@ def tile_linear_kernel(tc, q_weight, noise, alpha, fp_weight, offs, out):
         tc.tile_pool(name="held", bufs=1) as held,
         tc.tile_pool(name="blocks", bufs=BLOCKS) as blocks,
     ):
-        offsets = held.tile([P, N // 16], U16, name="offsets")
-        nc.sync.dma_start(offsets[:], offs)
         alpha_t = held.tile([P, BLOCKS], F32, name="alpha_t")
         nc.sync.dma_start(alpha_t[:], alpha.rearrange("(p n) one -> p (n one)", n=BLOCKS))
         outliers = held.tile([P, BLOCKS * N], F32, name="outliers")
+        offsets = held.tile([P, N // 16], U16, name="offsets")
+        q_tiles = []
+        z_tiles = []
+        for n in range(BLOCKS):
+            q = blocks.tile([P, S], F32, name="q")
+            z = blocks.tile([P, S], F32, name="z")
+            for cols in column_pieces(n):
+                nc.sync.dma_start(q[:, cols], q_rows[:, n, cols])
+                nc.sync.dma_start(z[:, cols], noise_rows[:, n, cols])
+            q_tiles.append(q)
+            z_tiles.append(z)
+            if n == 1:
+                nc.sync.dma_start(offsets[:], offs)
+                nc.sync.dma_start(outliers[:], fp_weight.rearrange("(p n) j -> p (n j)", n=BLOCKS))
 
         neg_alpha = held.tile([P, BLOCKS], F32, name="neg_alpha")
         nc.vector.tensor_scalar_mul(neg_alpha[:], alpha_t[:], -1.0)
         half_step = held.tile([P, BLOCKS], F32, name="half_step")
         nc.vector.tensor_scalar_mul(half_step[:], alpha_t[:], HALF_STEP)
 
-        q_tiles = []
-        z_tiles = []
-        for n in range(BLOCKS):
-            q = blocks.tile([P, S], F32, name="q")
-            nc.sync.dma_start(q[:], q_rows[:, n, :])
-            q_tiles.append(q)
-            z = blocks.tile([P, S], F32, name="z")
-            nc.sync.dma_start(z[:], noise_rows[:, n, :])
-            z_tiles.append(z)
-            if n == 0:
-                nc.sync.dma_start(outliers[:], fp_weight.rearrange("(p n) j -> p (n j)", n=BLOCKS))
-
         for n in range(BLOCKS):
             a = alpha_t[:, n : n + 1]
             q = q_tiles[n]
             z = z_tiles[n]
-
             q_abs = blocks.tile([P, S], F32, name="q_abs")
-            nc.scalar.activation(q_abs[:], q[:], ACT.Abs)
             clipped = blocks.tile([P, S], F32, name="clipped")
-            nc.vector.tensor_scalar(clipped[:], q[:], a, neg_alpha[:, n : n + 1], ALU.min, ALU.max)
             kept = blocks.tile([P, S], F32, name="kept")
-            nc.vector.scalar_tensor_tensor(kept[:], q_abs[:], a, z[:], ALU.is_lt, ALU.mult)
             wn = blocks.tile([P, S], F32, name="wn")
-            nc.vector.scalar_tensor_tensor(
-                wn[:], kept[:], half_step[:, n : n + 1], clipped[:], ALU.mult, ALU.add
-            )
+
+            for cols in column_pieces(n):
+                nc.scalar.activation(q_abs[:, cols], q[:, cols], ACT.Abs)
+                nc.vector.tensor_scalar(
+                    clipped[:, cols], q[:, cols], a, neg_alpha[:, n : n + 1], ALU.min, ALU.max
+                )
+                nc.vector.scalar_tensor_tensor(
+                    kept[:, cols], q_abs[:, cols], a, z[:, cols], ALU.is_lt, ALU.mult
+                )
+                nc.vector.scalar_tensor_tensor(
+                    wn[:, cols], kept[:, cols], half_step[:, n : n + 1], clipped[:, cols], ALU.mult, ALU.add
+                )
 
             nc.scalar.activation(wn[:].indirect(offsets[:]), outliers[:, n * N : (n + 1) * N], ACT.Copy)
             nc.sync.dma_start(out_rows[:, n, :], wn[:])

@@ -63,7 +63,7 @@ def tile_linear_kernel(tc, q_weight, noise, alpha, fp_weight, offs, out):
 
             for cols in column_pieces(n):
                 nc.scalar.activation(q_abs[:, cols], q[:, cols], ACT.Abs)
-                nc.vector.tensor_scalar(
+                nc.gpsimd.tensor_scalar(
                     clipped[:, cols], q[:, cols], a, neg_alpha[:, n : n + 1], ALU.min, ALU.max
                 )
                 nc.vector.scalar_tensor_tensor(

@@ -9,13 +9,13 @@ P = 128
 C, S, N = 512, 1024, 128
 BLOCKS = C // P
 HALF_STEP = 0.5 / 7.0
-FIRST_BLOCK_EDGES = (0, S // 4, S // 2, S)
-BLOCK_EDGES = (0, S)
+FIRST_BLOCK_PIECES = 4
 
 
 def column_pieces(n):
-    edges = FIRST_BLOCK_EDGES if n == 0 else BLOCK_EDGES
-    return [slice(lo, hi) for lo, hi in zip(edges[:-1], edges[1:])]
+    pieces = max(1, FIRST_BLOCK_PIECES >> n)
+    width = S // pieces
+    return [slice(k * width, (k + 1) * width) for k in range(pieces)]
 
 
 def tile_linear_kernel(tc, q_weight, noise, alpha, fp_weight, offs, out):
@@ -43,7 +43,7 @@ def tile_linear_kernel(tc, q_weight, noise, alpha, fp_weight, offs, out):
                 nc.sync.dma_start(z[:, cols], noise_rows[:, n, cols])
             q_tiles.append(q)
             z_tiles.append(z)
-            if n == 1:
+            if n == BLOCKS - 1:
                 nc.sync.dma_start(offsets[:], offs)
                 nc.sync.dma_start(outliers[:], fp_weight.rearrange("(p n) j -> p (n j)", n=BLOCKS))
 
@@ -63,7 +63,7 @@ def tile_linear_kernel(tc, q_weight, noise, alpha, fp_weight, offs, out):
 
             for cols in column_pieces(n):
                 nc.scalar.activation(q_abs[:, cols], q[:, cols], ACT.Abs)
-                nc.gpsimd.tensor_scalar(
+                nc.vector.tensor_scalar(
                     clipped[:, cols], q[:, cols], a, neg_alpha[:, n : n + 1], ALU.min, ALU.max
                 )
                 nc.vector.scalar_tensor_tensor(

@@ -40,12 +40,12 @@ def tile_linear_kernel(tc, q_weight, noise, alpha, fp_weight, offs, out):
             z = blocks.tile([P, S], F32, name="z")
             for cols in column_pieces(n):
                 nc.sync.dma_start(q[:, cols], q_rows[:, n, cols])
+                if n == BLOCKS - 1:
+                    nc.sync.dma_start(offsets[:], offs)
+                    nc.sync.dma_start(outliers[:], fp_weight.rearrange("(p n) j -> p (n j)", n=BLOCKS))
                 nc.sync.dma_start(z[:, cols], noise_rows[:, n, cols])
             q_tiles.append(q)
             z_tiles.append(z)
-            if n == BLOCKS - 1:
-                nc.sync.dma_start(offsets[:], offs)
-                nc.sync.dma_start(outliers[:], fp_weight.rearrange("(p n) j -> p (n j)", n=BLOCKS))
 
         neg_alpha = held.tile([P, BLOCKS], F32, name="neg_alpha")
         nc.vector.tensor_scalar_mul(neg_alpha[:], alpha_t[:], -1.0)

@@ -74,4 +74,4 @@ def tile_linear_kernel(tc, q_weight, noise, alpha, fp_weight, offs, out):
                 )
 
             nc.scalar.activation(wn[:].indirect(offsets[:]), outliers[:, n * N : (n + 1) * N], ACT.Copy)
-            nc.sync.dma_start(out_rows[:, n, :], wn[:])
+            nc.scalar.dma_start(out_rows[:, n, :], wn[:])

@@ -30,7 +30,7 @@ def tile_linear_kernel(tc, q_weight, noise, alpha, fp_weight, offs, out):
         tc.tile_pool(name="blocks", bufs=BLOCKS) as blocks,
     ):
         alpha_t = held.tile([P, BLOCKS], F32, name="alpha_t")
-        nc.sync.dma_start(alpha_t[:], alpha.rearrange("(p n) one -> p (n one)", n=BLOCKS))
+        nc.scalar.dma_start(alpha_t[:], alpha.rearrange("(p n) one -> p (n one)", n=BLOCKS))
         outliers = held.tile([P, BLOCKS * N], F32, name="outliers")
         offsets = held.tile([P, N // 16], U16, name="offsets")
         q_tiles = []
@@ -38,12 +38,15 @@ def tile_linear_kernel(tc, q_weight, noise, alpha, fp_weight, offs, out):
         for n in range(BLOCKS):
             q = blocks.tile([P, S], F32, name="q")
             z = blocks.tile([P, S], F32, name="z")
-            for cols in column_pieces(n):
-                nc.sync.dma_start(q[:, cols], q_rows[:, n, cols])
+            pieces = column_pieces(n)
+            for k in range(0, len(pieces), 2):
+                for cols in pieces[k : k + 2]:
+                    nc.sync.dma_start(q[:, cols], q_rows[:, n, cols])
                 if n == BLOCKS - 1:
                     nc.sync.dma_start(offsets[:], offs)
                     nc.sync.dma_start(outliers[:], fp_weight.rearrange("(p n) j -> p (n j)", n=BLOCKS))
-                nc.sync.dma_start(z[:, cols], noise_rows[:, n, cols])
+                for cols in pieces[k : k + 2]:
+                    nc.sync.dma_start(z[:, cols], noise_rows[:, n, cols])
             q_tiles.append(q)
             z_tiles.append(z)
 

@@ -55,26 +55,34 @@ def tile_linear_kernel(tc, q_weight, noise, alpha, fp_weight, offs, out):
         half_step = held.tile([P, BLOCKS], F32, name="half_step")
         nc.vector.tensor_scalar_mul(half_step[:], alpha_t[:], HALF_STEP)
 
-        for n in range(BLOCKS):
+        q_abs_tiles = [blocks.tile([P, S], F32, name="q_abs") for n in range(BLOCKS)]
+        clipped_tiles = [blocks.tile([P, S], F32, name="clipped") for n in range(BLOCKS)]
+        kept_tiles = [blocks.tile([P, S], F32, name="kept") for n in range(BLOCKS)]
+        wn_tiles = [blocks.tile([P, S], F32, name="wn") for n in range(BLOCKS)]
+
+        def clip_and_mask(n, cols):
             a = alpha_t[:, n : n + 1]
-            q = q_tiles[n]
-            z = z_tiles[n]
-            q_abs = blocks.tile([P, S], F32, name="q_abs")
-            clipped = blocks.tile([P, S], F32, name="clipped")
-            kept = blocks.tile([P, S], F32, name="kept")
-            wn = blocks.tile([P, S], F32, name="wn")
+            nc.scalar.activation(q_abs_tiles[n][:, cols], q_tiles[n][:, cols], ACT.Abs)
+            nc.vector.tensor_scalar(
+                clipped_tiles[n][:, cols], q_tiles[n][:, cols], a, neg_alpha[:, n : n + 1], ALU.min, ALU.max
+            )
+            nc.vector.scalar_tensor_tensor(
+                kept_tiles[n][:, cols], q_abs_tiles[n][:, cols], a, z_tiles[n][:, cols], ALU.is_lt, ALU.mult
+            )
 
-            for cols in column_pieces(n):
-                nc.scalar.activation(q_abs[:, cols], q[:, cols], ACT.Abs)
-                nc.vector.tensor_scalar(
-                    clipped[:, cols], q[:, cols], a, neg_alpha[:, n : n + 1], ALU.min, ALU.max
-                )
-                nc.vector.scalar_tensor_tensor(
-                    kept[:, cols], q_abs[:, cols], a, z[:, cols], ALU.is_lt, ALU.mult
-                )
-                nc.vector.scalar_tensor_tensor(
-                    wn[:, cols], kept[:, cols], half_step[:, n : n + 1], clipped[:, cols], ALU.mult, ALU.add
-                )
+        def add_noise(n, cols):
+            wn = wn_tiles[n]
+            nc.vector.scalar_tensor_tensor(
+                wn[:, cols], kept_tiles[n][:, cols], half_step[:, n : n + 1], clipped_tiles[n][:, cols],
+                ALU.mult, ALU.add,
+            )
+            if cols.stop == S:
+                nc.scalar.activation(wn[:].indirect(offsets[:]), outliers[:, n * N : (n + 1) * N], ACT.Copy)
+                nc.scalar.dma_start(out_rows[:, n, :], wn[:])
 
-            nc.scalar.activation(wn[:].indirect(offsets[:]), outliers[:, n * N : (n + 1) * N], ACT.Copy)
-            nc.scalar.dma_start(out_rows[:, n, :], wn[:])
+        work = [(n, cols) for n in range(BLOCKS) for cols in column_pieces(n)]
+        for step in range(len(work) + 1):
+            if step < len(work):
+                clip_and_mask(*work[step])
+            if step > 0:
+                add_noise(*work[step - 1])

@@ -30,7 +30,7 @@ def tile_linear_kernel(tc, q_weight, noise, alpha, fp_weight, offs, out):
         tc.tile_pool(name="blocks", bufs=BLOCKS) as blocks,
     ):
         alpha_t = held.tile([P, BLOCKS], F32, name="alpha_t")
-        nc.scalar.dma_start(alpha_t[:], alpha.rearrange("(p n) one -> p (n one)", n=BLOCKS))
+        nc.sync.dma_start(alpha_t[:], alpha.rearrange("(p n) one -> p (n one)", n=BLOCKS))
         outliers = held.tile([P, BLOCKS * N], F32, name="outliers")
         offsets = held.tile([P, N // 16], U16, name="offsets")
         q_tiles = []

import concourse.mybir as mybir

F32 = mybir.dt.float32
U16 = mybir.dt.uint16
ALU = mybir.AluOpType
ACT = mybir.ActivationFunctionType

P = 128
C, S, N = 512, 1024, 128
BLOCKS = C // P
HALF_STEP = 0.5 / 7.0
FIRST_BLOCK_PIECES = 4


def column_pieces(n):
    pieces = max(1, FIRST_BLOCK_PIECES >> n)
    width = S // pieces
    return [slice(k * width, (k + 1) * width) for k in range(pieces)]


def tile_linear_kernel(tc, q_weight, noise, alpha, fp_weight, offs, out):
    nc = tc.nc

    q_rows = q_weight.rearrange("(p n) s -> p n s", n=BLOCKS)
    noise_rows = noise.rearrange("(p n) s -> p n s", n=BLOCKS)
    out_rows = out.rearrange("(p n) s -> p n s", n=BLOCKS)

    with (
        tc.tile_pool(name="held", bufs=1) as held,
        tc.tile_pool(name="blocks", bufs=BLOCKS) as blocks,
    ):
        alpha_t = held.tile([P, BLOCKS], F32, name="alpha_t")
        nc.sync.dma_start(alpha_t[:], alpha.rearrange("(p n) one -> p (n one)", n=BLOCKS))
        outliers = held.tile([P, BLOCKS * N], F32, name="outliers")
        offsets = held.tile([P, N // 16], U16, name="offsets")
        q_tiles = []
        z_tiles = []
        for n in range(BLOCKS):
            q = blocks.tile([P, S], F32, name="q")
            z = blocks.tile([P, S], F32, name="z")
            pieces = column_pieces(n)
            for k in range(0, len(pieces), 2):
                for cols in pieces[k : k + 2]:
                    nc.sync.dma_start(q[:, cols], q_rows[:, n, cols])
                if n == BLOCKS - 1:
                    nc.sync.dma_start(offsets[:], offs)
                    nc.sync.dma_start(outliers[:], fp_weight.rearrange("(p n) j -> p (n j)", n=BLOCKS))
                for cols in pieces[k : k + 2]:
                    nc.sync.dma_start(z[:, cols], noise_rows[:, n, cols])
            q_tiles.append(q)
            z_tiles.append(z)

        neg_alpha = held.tile([P, BLOCKS], F32, name="neg_alpha")
        nc.vector.tensor_scalar_mul(neg_alpha[:], alpha_t[:], -1.0)
        half_step = held.tile([P, BLOCKS], F32, name="half_step")
        nc.vector.tensor_scalar_mul(half_step[:], alpha_t[:], HALF_STEP)

        q_abs_tiles = [blocks.tile([P, S], F32, name="q_abs") for n in range(BLOCKS)]
        clipped_tiles = [blocks.tile([P, S], F32, name="clipped") for n in range(BLOCKS)]
        kept_tiles = [blocks.tile([P, S], F32, name="kept") for n in range(BLOCKS)]
        wn_tiles = [blocks.tile([P, S], F32, name="wn") for n in range(BLOCKS)]

        def clip_and_mask(n, cols):
            a = alpha_t[:, n : n + 1]
            nc.scalar.activation(q_abs_tiles[n][:, cols], q_tiles[n][:, cols], ACT.Abs)
            nc.vector.tensor_scalar(
                clipped_tiles[n][:, cols], q_tiles[n][:, cols], a, neg_alpha[:, n : n + 1], ALU.min, ALU.max
            )
            nc.vector.scalar_tensor_tensor(
                kept_tiles[n][:, cols], q_abs_tiles[n][:, cols], a, z_tiles[n][:, cols], ALU.is_lt, ALU.mult
            )

        def add_noise(n, cols):
            wn = wn_tiles[n]
            nc.vector.scalar_tensor_tensor(
                wn[:, cols], kept_tiles[n][:, cols], half_step[:, n : n + 1], clipped_tiles[n][:, cols],
                ALU.mult, ALU.add,
            )
            if cols.stop == S:
                nc.scalar.activation(wn[:].indirect(offsets[:]), outliers[:, n * N : (n + 1) * N], ACT.Copy)
                nc.scalar.dma_start(out_rows[:, n, :], wn[:])

        work = [(n, cols) for n in range(BLOCKS) for cols in column_pieces(n)]
        for step in range(len(work) + 1):
            if step < len(work):
                clip_and_mask(*work[step])
            if step > 0:
                add_noise(*work[step - 1])
